import numpy as np
import ml_dtypes


def mxq(x, axis, fmt="e4m3"):
    dtype, down = {"e4m3": (ml_dtypes.float8_e4m3fn, 7), "e5m2": (ml_dtypes.float8_e5m2, 14)}[fmt]
    v = np.moveaxis(np.asarray(x, np.float32).astype(ml_dtypes.bfloat16).astype(np.float64), axis, -1)
    blocks = v.reshape(v.shape[:-1] + (-1, 32))
    amax = np.abs(blocks).max(-1, keepdims=True)
    byte = np.maximum(np.where(amax > 0, np.frexp(amax)[1] - 1 + 127, 0) - down, 1)
    scale = np.exp2(byte - 127.0)
    codes = (blocks / scale).astype(np.float32).astype(dtype).astype(np.float64)
    return np.moveaxis((codes * scale).reshape(v.shape), -1, axis)


WIDE = False


def mx_kscale(k):
    if not WIDE:
        return np.ones(k)
    levels = np.array([10, -10, 5, -5, 0])
    a = np.random.permutation(np.resize(levels, k // 512 * 4)).reshape(k // 512, 4)
    idx = np.arange(k)
    return np.exp2(a[idx // 512, idx % 128 // 32])


BF16 = ml_dtypes.bfloat16


def bf(x):
    return np.asarray(x, np.float32).astype(BF16)


def f64(x):
    return np.asarray(x).astype(np.float64)


B, SIDE, HE, Z, HD, XO = 4096, 32, 1024, 512, 1024, 512


def setup_inputs():
    n = np.random.standard_normal
    s = mx_kscale(HD)
    return {"hd": bf(np.tanh(n((B, HD))) * s),
            "W_mu_d": bf(n((XO, HD)) * 1.5 / np.sqrt(HD) / s[None, :]),
            "b_mu_d": bf(n(XO) * 0.3),
            "W_ls_d": bf(n((XO, HD)) * 1.5 / np.sqrt(HD) / s[None, :]),
            "b_ls_d": bf(n(XO) * 0.3),
            "eps_x": bf(n((B, XO)))}


def reference(hd, W_mu_d, b_mu_d, W_ls_d, b_ls_d, eps_x):
    hq = mxq(f64(hd), 1, "e4m3")
    mu_d = (hq @ mxq(f64(W_mu_d), 1, "e4m3").T) + f64(b_mu_d)
    ls_d = (hq @ mxq(f64(W_ls_d), 1, "e4m3").T) + f64(b_ls_d)
    return mu_d + np.exp(0.5 * ls_d) * f64(eps_x)

@@ -1,0 +1,185 @@
+from contextlib import ExitStack
+
+import concourse.mybir as mybir
+from concourse.masks import make_identity
+
+F32 = mybir.dt.float32
+BF16 = mybir.dt.bfloat16
+U32 = mybir.dt.uint32
+U8 = mybir.dt.uint8
+FP8X4 = mybir.dt.float8_e4m3fn_x4
+ACT = mybir.ActivationFunctionType
+ALU = mybir.AluOpType
+
+P = 128
+B, K, XO = 4096, 1024, 512
+T4 = 4
+GROUPS = B // (P * T4)
+PASSES = K // 512
+FLOPS = 2 * B * K * 2 * XO
+
+
+def tile_vae_pb_t_kernel(tc, hd, W_mu_d, b_mu_d, W_ls_d, b_ls_d, eps_x, out):
+    nc = tc.nc
+    hd_v = hd.rearrange("(g p i) k -> g p (i k)", p=P, i=T4)
+    eps_v = eps_x.rearrange("(g p i) n -> g p (i n)", p=P, i=T4)
+    out_v = out.rearrange("(g p i) n -> g p (i n)", p=P, i=T4)
+
+    with ExitStack() as ctx:
+        const = ctx.enter_context(tc.tile_pool(name="const", bufs=1))
+        raw = ctx.enter_context(tc.tile_pool(name="raw", bufs=6))
+        epsp = ctx.enter_context(tc.tile_pool(name="epsp", bufs=GROUPS))
+        grpp = ctx.enter_context(tc.tile_pool(name="grpp", bufs=2))
+        hcp = ctx.enter_context(tc.tile_pool(name="hcp", bufs=3))
+        etp = ctx.enter_context(tc.tile_pool(name="etp", bufs=4))
+        upp = ctx.enter_context(tc.tile_pool(name="upp", bufs=2))
+        outp = ctx.enter_context(tc.tile_pool(name="outp", bufs=4))
+        psum = ctx.enter_context(tc.psum_pool(name="psum", bufs=1))
+
+        def bank(tag, shape, dtype=F32):
+            return psum.tile(shape, dtype, tag=tag, name="ps" + tag)
+
+        ident = const.tile([P, P], F32, name="ident")
+        make_identity(nc, ident[:])
+        ident_bf = const.tile([P, P], BF16, name="ident_bf")
+        make_identity(nc, ident_bf[:])
+        ones = const.tile([P, P], BF16, name="ones")
+        nc.vector.memset(ones[:], 1.0)
+        brow = const.tile([P, XO], BF16, name="brow")
+        nc.vector.memset(brow[:], 0.0)
+        bcol = const.tile([P, P], BF16, name="bcol")
+        nc.vector.memset(bcol[:], 0.0)
+        warm = const.tile([P, 1], F32, name="warm")
+        nc.vector.memset(warm[:], 0.0)
+        warm2 = const.tile([P, 1], F32, name="warm2")
+        nc.scalar.activation(out=warm2[:], in_=warm[:], func=ACT.Exp)
+        nc.scalar.dma_start(out=brow[0:1, :], in_=b_mu_d.rearrange("(o n) -> o n", o=1))
+        nc.scalar.dma_start(out=bcol[0:T4, :], in_=b_ls_d.rearrange("(j q) -> j q", q=P))
+
+        def load_w(w, nm):
+            t = raw.tile([P, T4 * K], BF16, tag="raw", name=nm)
+            nc.sync.dma_start(
+                out=t[:].rearrange("q (r k) -> q r k", r=T4),
+                in_=w.rearrange("(r q) k -> q r k", q=P),
+            )
+            return t
+
+        hd_sb = {}
+        eps_sb = {}
+
+        def load_hd(g):
+            t = raw.tile([P, T4 * K], BF16, tag="raw", name="hd_sb")
+            nc.sync.dma_start(out=t[:], in_=hd_v[g])
+            hd_sb[g] = t
+
+        def load_eps(g):
+            t = epsp.tile([P, T4 * XO], BF16, tag="eps", name="eps_sb")
+            nc.sync.dma_start(out=t[:], in_=eps_v[g])
+            eps_sb[g] = t
+
+        wls_sb = load_w(W_ls_d, "wls_sb")
+        load_hd(0)
+        wmu_sb = load_w(W_mu_d, "wmu_sb")
+        load_hd(1)
+        load_eps(0)
+        for g in range(2, GROUPS):
+            load_hd(g)
+            load_eps(g - 1)
+        load_eps(GROUPS - 1)
+
+        c_ps = bank("B0", [P, XO])
+        nc.tensor.matmul(out=c_ps[:], lhsT=ones[:], rhs=brow[:], start=True, stop=True)
+        c_bc = const.tile([P, XO], F32, name="c_bc")
+        nc.vector.tensor_copy(out=c_bc[:], in_=c_ps[:])
+        bt_ps = bank("B1", [P, P], BF16)
+        nc.tensor.transpose(bt_ps[:], bcol[:], ident_bf[:])
+        half_bls = const.tile([P, T4], F32, name="half_bls")
+        nc.vector.tensor_scalar_mul(out=half_bls[:], in0=bt_ps[:, 0:T4], scalar1=0.5)
+
+        def transposes(src, side):
+            words = src[:].bitcast(F32)
+            banks = []
+            for i in range(T4):
+                bk = bank(side + str(i), [P, 4, P])
+                for s in range(4):
+                    c0 = i * 512 + s * P
+                    nc.tensor.transpose(bk[:, s, :], words[:, c0 : c0 + P], ident[:])
+                banks.append(bk)
+            return banks
+
+        def regroup(banks, engines):
+            grp = grpp.tile([P, T4 * K], BF16, tag="grp", name="grp", align_bytes=64)
+            gw = grp[:].bitcast(F32).rearrange("p (g c u) -> p g c u", g=PASSES, u=2)
+            for i in range(T4):
+                dst = gw[:, :, i * P : (i + 1) * P, :]
+                src = banks[i][:].rearrange("p (g u) b -> p g b u", u=2)
+                if engines[i] == "v":
+                    nc.vector.tensor_copy(out=dst, in_=src)
+                else:
+                    nc.scalar.copy(out=dst, in_=src)
+            return grp
+
+        def quantise(grp, pool, tag):
+            codes = pool.tile([P, PASSES * 512], U32, tag=tag + "c", name=tag + "c", align_bytes=64)
+            scales = pool.tile([P, PASSES * 512], U8, tag=tag + "s", name=tag + "s", align_bytes=64)
+            nc.vector.quantize_mx(out=codes[:].bitcast(FP8X4), scales=scales[:], in_=grp[:])
+            return codes, scales
+
+        def mx(acc, stat, s0, mov, m0, n):
+            for c in range(PASSES):
+                a = c * 512 + s0
+                b = c * 512 + m0
+                nc.tensor.matmul_mx(
+                    out=acc,
+                    lhsT=stat[0][:, a : a + P].bitcast(FP8X4),
+                    lhsT_scale=stat[1][:, a : a + P],
+                    rhs=mov[0][:, b : b + n].bitcast(FP8X4),
+                    rhs_scale=mov[1][:, b : b + n],
+                    start=(c == 0),
+                    stop=(c == PASSES - 1),
+                )
+
+        wls_q = quantise(regroup(transposes(wls_sb, "A"), "vsvs"), const, "wls")
+        hq = {}
+        hq[0] = quantise(regroup(transposes(hd_sb[0], "B"), "vsvs"), hcp, "h")
+        wmu_q = quantise(regroup(transposes(wmu_sb, "A"), "vsvs"), const, "wmu")
+        pending = transposes(hd_sb[1], "B")
+
+        for g in range(GROUPS):
+            if g + 1 < GROUPS:
+                grp_next = regroup(pending, "ssss")
+            ls_banks = []
+            for j in range(T4):
+                acc = bank("A" + str(j), [P, 512])
+                mx(acc[:], wls_q, j * P, hq[g], 0, 512)
+                ls_banks.append(acc)
+            if g + 1 < GROUPS:
+                hq[g + 1] = quantise(grp_next, hcp, "h")
+            ets = []
+            for j in range(T4):
+                et = etp.tile([P, 512], F32, tag="et", name="et")
+                nc.scalar.activation(
+                    out=et[:], in_=ls_banks[j][:], func=ACT.Exp, bias=half_bls[:, j : j + 1], scale=0.5
+                )
+                ets.append(et)
+            u = upp.tile([P, T4 * XO], F32, tag="u", name="u")
+            for i in range(T4):
+                acc = bank("B" + str(i), [P, XO])
+                mx(acc[:], hq[g], i * P, wmu_q, 0, XO)
+                nc.vector.tensor_tensor(out=u[:, i * XO : (i + 1) * XO], in0=acc[:], in1=c_bc[:], op=ALU.add)
+            prod = upp.tile([P, T4 * XO], F32, tag="prod", name="prod")
+            res = outp.tile([P, T4 * XO], F32, tag="res", name="res")
+            u3 = u[:].rearrange("p (i n) -> p i n", i=T4)
+            p3 = prod[:].rearrange("p (i n) -> p i n", i=T4)
+            r3 = res[:].rearrange("p (i n) -> p i n", i=T4)
+            e3 = eps_sb[g][:].rearrange("p (i n) -> p i n", i=T4)
+            for j in range(T4):
+                eb = bank("A" + str(j), [P, T4, P])
+                for i in range(T4):
+                    nc.tensor.transpose(eb[:, i, :], ets[j][:, i * P : (i + 1) * P], ident[:])
+                cols = slice(j * P, (j + 1) * P)
+                nc.vector.tensor_tensor(out=p3[:, :, cols], in0=eb[:], in1=e3[:, :, cols], op=ALU.mult)
+                nc.gpsimd.tensor_tensor(out=r3[:, :, cols], in0=u3[:, :, cols], in1=p3[:, :, cols], op=ALU.add)
+            nc.sync.dma_start(out=out_v[g], in_=res[:])
+            if g + 2 < GROUPS:
+                pending = transposes(hd_sb[g + 2], "B")

@@ -17,24 +17,30 @@ T4 = 4
 GROUPS = B // (P * T4)
 PASSES = K // 512
 FLOPS = 2 * B * K * 2 * XO
+MODES = "HHHHHHHH"
+PROD_ON_V = 2
 
 
 def tile_vae_pb_t_kernel(tc, hd, W_mu_d, b_mu_d, W_ls_d, b_ls_d, eps_x, out):
     nc = tc.nc
     hd_v = hd.rearrange("(g p i) k -> g p (i k)", p=P, i=T4)
+    hd_pieces = hd.rearrange("(g p i) k -> g i p k", p=P, i=T4)
     eps_v = eps_x.rearrange("(g p i) n -> g p (i n)", p=P, i=T4)
     out_v = out.rearrange("(g p i) n -> g p (i n)", p=P, i=T4)
+    out_v3 = out.rearrange("(g p i) n -> g p i n", p=P, i=T4)
 
     with ExitStack() as ctx:
         const = ctx.enter_context(tc.tile_pool(name="const", bufs=1))
-        raw = ctx.enter_context(tc.tile_pool(name="raw", bufs=6))
+        raw = ctx.enter_context(tc.tile_pool(name="raw", bufs=4))
         epsp = ctx.enter_context(tc.tile_pool(name="epsp", bufs=GROUPS))
         grpp = ctx.enter_context(tc.tile_pool(name="grpp", bufs=2))
+        grpw = ctx.enter_context(tc.tile_pool(name="grpw", bufs=4))
         hcp = ctx.enter_context(tc.tile_pool(name="hcp", bufs=3))
         etp = ctx.enter_context(tc.tile_pool(name="etp", bufs=4))
         upp = ctx.enter_context(tc.tile_pool(name="upp", bufs=2))
         outp = ctx.enter_context(tc.tile_pool(name="outp", bufs=4))
         psum = ctx.enter_context(tc.psum_pool(name="psum", bufs=1))
+        ctx.enter_context(tc.manual_schedule())
 
         def bank(tag, shape, dtype=F32):
             return psum.tile(shape, dtype, tag=tag, name="ps" + tag)
@@ -43,92 +49,92 @@ def tile_vae_pb_t_kernel(tc, hd, W_mu_d, b_mu_d, W_ls_d, b_ls_d, eps_x, out):
         make_identity(nc, ident[:])
         ident_bf = const.tile([P, P], BF16, name="ident_bf")
         make_identity(nc, ident_bf[:])
-        ones = const.tile([P, P], BF16, name="ones")
-        nc.vector.memset(ones[:], 1.0)
-        brow = const.tile([P, XO], BF16, name="brow")
-        nc.vector.memset(brow[:], 0.0)
+        brow_mu = const.tile([P, XO], BF16, name="brow_mu")
+        nc.vector.memset(brow_mu[:], 0.0)
+        brow_ls = const.tile([P, XO], BF16, name="brow_ls")
+        nc.vector.memset(brow_ls[:], 0.0)
         bcol = const.tile([P, P], BF16, name="bcol")
         nc.vector.memset(bcol[:], 0.0)
+        ones = const.tile([P, P], BF16, name="ones")
+        nc.vector.memset(ones[:], 1.0)
         warm = const.tile([P, 1], F32, name="warm")
         nc.vector.memset(warm[:], 0.0)
+        nc.scalar.dma_start(out=bcol[0:T4, :], in_=b_ls_d.rearrange("(j q) -> j q", q=P))
+        nc.scalar.dma_start(out=brow_mu[0:1, :], in_=b_mu_d.rearrange("(o n) -> o n", o=1))
+        nc.scalar.dma_start(out=brow_ls[0:1, :], in_=b_ls_d.rearrange("(o n) -> o n", o=1))
         warm2 = const.tile([P, 1], F32, name="warm2")
         nc.scalar.activation(out=warm2[:], in_=warm[:], func=ACT.Exp)
-        nc.scalar.dma_start(out=brow[0:1, :], in_=b_mu_d.rearrange("(o n) -> o n", o=1))
-        nc.scalar.dma_start(out=bcol[0:T4, :], in_=b_ls_d.rearrange("(j q) -> j q", q=P))
-
-        def load_w(w, nm):
-            t = raw.tile([P, T4 * K], BF16, tag="raw", name=nm)
-            nc.sync.dma_start(
-                out=t[:].rearrange("q (r k) -> q r k", r=T4),
-                in_=w.rearrange("(r q) k -> q r k", q=P),
-            )
-            return t
 
         hd_sb = {}
         eps_sb = {}
 
-        def load_hd(g):
+        def load_hd(g, pieces):
             t = raw.tile([P, T4 * K], BF16, tag="raw", name="hd_sb")
-            nc.sync.dma_start(out=t[:], in_=hd_v[g])
+            if pieces:
+                for i in range(T4):
+                    nc.sync.dma_start(out=t[:, i * K : (i + 1) * K], in_=hd_pieces[g, i])
+            else:
+                nc.sync.dma_start(out=t[:], in_=hd_v[g])
             hd_sb[g] = t
+
+        def load_w(w, nm):
+            t = const.tile([P, T4 * K], BF16, name=nm)
+            for r in range(T4):
+                nc.sync.dma_start(out=t[:, r * K : (r + 1) * K], in_=w[r * P : (r + 1) * P, :])
+            return t
 
         def load_eps(g):
             t = epsp.tile([P, T4 * XO], BF16, tag="eps", name="eps_sb")
             nc.sync.dma_start(out=t[:], in_=eps_v[g])
             eps_sb[g] = t
 
+        load_hd(0, True)
         wls_sb = load_w(W_ls_d, "wls_sb")
-        load_hd(0)
         wmu_sb = load_w(W_mu_d, "wmu_sb")
-        load_hd(1)
         load_eps(0)
+        load_hd(1, False)
         for g in range(2, GROUPS):
-            load_hd(g)
+            load_hd(g, False)
             load_eps(g - 1)
         load_eps(GROUPS - 1)
 
-        c_ps = bank("B0", [P, XO])
-        nc.tensor.matmul(out=c_ps[:], lhsT=ones[:], rhs=brow[:], start=True, stop=True)
-        c_bc = const.tile([P, XO], F32, name="c_bc")
-        nc.vector.tensor_copy(out=c_bc[:], in_=c_ps[:])
-        bt_ps = bank("B1", [P, P], BF16)
-        nc.tensor.transpose(bt_ps[:], bcol[:], ident_bf[:])
-        half_bls = const.tile([P, T4], F32, name="half_bls")
-        nc.vector.tensor_scalar_mul(out=half_bls[:], in0=bt_ps[:, 0:T4], scalar1=0.5)
-
-        def transposes(src, side):
+        def transpose_tile(src, i, tag):
             words = src[:].bitcast(F32)
-            banks = []
-            for i in range(T4):
-                bk = bank(side + str(i), [P, 4, P])
-                for s in range(4):
-                    c0 = i * 512 + s * P
-                    nc.tensor.transpose(bk[:, s, :], words[:, c0 : c0 + P], ident[:])
-                banks.append(bk)
-            return banks
+            bk = bank(tag, [P, 4, P])
+            for s in range(4):
+                c0 = i * 512 + s * P
+                nc.tensor.transpose(bk[:, s, :], words[:, c0 : c0 + P], ident[:])
+            return bk
 
-        def regroup(banks, engines):
-            grp = grpp.tile([P, T4 * K], BF16, tag="grp", name="grp", align_bytes=64)
+        def copy_out(eng, dst, bk):
+            src = bk[:].rearrange("p (g u) b -> p g b u", u=2)
+            if eng == "v":
+                nc.vector.tensor_copy(out=dst, in_=src)
+            else:
+                nc.scalar.copy(out=dst, in_=src)
+
+        def new_grp():
+            return grpp.tile([P, T4 * K], BF16, tag="grp", name="grp", align_bytes=64)
+
+        def grp_slot(grp, i):
             gw = grp[:].bitcast(F32).rearrange("p (g c u) -> p g c u", g=PASSES, u=2)
-            for i in range(T4):
-                dst = gw[:, :, i * P : (i + 1) * P, :]
-                src = banks[i][:].rearrange("p (g u) b -> p g b u", u=2)
-                if engines[i] == "v":
-                    nc.vector.tensor_copy(out=dst, in_=src)
-                else:
-                    nc.scalar.copy(out=dst, in_=src)
-            return grp
+            return gw[:, :, i * P : (i + 1) * P, :]
 
         def quantise(grp, pool, tag):
             codes = pool.tile([P, PASSES * 512], U32, tag=tag + "c", name=tag + "c", align_bytes=64)
             scales = pool.tile([P, PASSES * 512], U8, tag=tag + "s", name=tag + "s", align_bytes=64)
-            nc.vector.quantize_mx(out=codes[:].bitcast(FP8X4), scales=scales[:], in_=grp[:])
+            for c in range(PASSES):
+                nc.vector.quantize_mx(
+                    out=codes[:, c * 512 : (c + 1) * 512].bitcast(FP8X4),
+                    scales=scales[:, c * 512 : (c + 1) * 512],
+                    in_=grp[:, c * 2048 : (c + 1) * 2048],
+                )
             return codes, scales
 
-        def mx(acc, stat, s0, mov, m0, n):
+        def mx(acc, stat, s_pitch, s0, mov, m_pitch, m0, n):
             for c in range(PASSES):
-                a = c * 512 + s0
-                b = c * 512 + m0
+                a = c * s_pitch + s0
+                b = c * m_pitch + m0
                 nc.tensor.matmul_mx(
                     out=acc,
                     lhsT=stat[0][:, a : a + P].bitcast(FP8X4),
@@ -139,47 +145,191 @@ def tile_vae_pb_t_kernel(tc, hd, W_mu_d, b_mu_d, W_ls_d, b_ls_d, eps_x, out):
                     stop=(c == PASSES - 1),
                 )
 
-        wls_q = quantise(regroup(transposes(wls_sb, "A"), "vsvs"), const, "wls")
         hq = {}
-        hq[0] = quantise(regroup(transposes(hd_sb[0], "B"), "vsvs"), hcp, "h")
-        wmu_q = quantise(regroup(transposes(wmu_sb, "A"), "vsvs"), const, "wmu")
-        pending = transposes(hd_sb[1], "B")
+        wls_q = {}
 
-        for g in range(GROUPS):
-            if g + 1 < GROUPS:
-                grp_next = regroup(pending, "ssss")
-            ls_banks = []
-            for j in range(T4):
-                acc = bank("A" + str(j), [P, 512])
-                mx(acc[:], wls_q, j * P, hq[g], 0, 512)
-                ls_banks.append(acc)
-            if g + 1 < GROUPS:
-                hq[g + 1] = quantise(grp_next, hcp, "h")
+        grp0 = new_grp()
+        for i in range(T4):
+            copy_out("vs"[i % 2], grp_slot(grp0, i), transpose_tile(hd_sb[0], i, "B" + str(i)))
+        hq[0] = quantise(grp0, hcp, "h")
+
+        wls_grp = []
+        for r in range(T4):
+            gt = grpw.tile([P, K], BF16, tag="grpw", name="grpw", align_bytes=64)
+            dst = gt[:].bitcast(F32).rearrange("p (g c u) -> p g c u", g=PASSES, u=2)
+            copy_out("s", dst, transpose_tile(wls_sb, r, "A" + str(r)))
+            wls_grp.append(gt)
+
+        bt_ps = bank("B0", [P, P], BF16)
+        nc.tensor.transpose(bt_ps[:], bcol[:], ident_bf[:])
+        c_ps = bank("B1", [P, XO])
+        nc.tensor.matmul(out=c_ps[:], lhsT=ones[:], rhs=brow_mu[:], start=True, stop=True)
+        l_ps = bank("B2", [P, XO])
+        nc.tensor.matmul(out=l_ps[:], lhsT=ones[:], rhs=brow_ls[:], start=True, stop=True)
+        half_bls = const.tile([P, T4], F32, name="half_bls")
+        c_bc = const.tile([P, XO], F32, name="c_bc")
+        bls_bc = const.tile([P, XO], F32, name="bls_bc")
+
+        def quantise_wls(r):
+            codes = const.tile([P, PASSES * P], U32, name="wlsc" + str(r), align_bytes=64)
+            scales = const.tile([P, PASSES * P], U8, name="wlss" + str(r), align_bytes=64)
+            nc.vector.quantize_mx(out=codes[:].bitcast(FP8X4), scales=scales[:], in_=wls_grp[r][:])
+            wls_q[r] = (codes, scales)
+
+        quantise_wls(0)
+        quantise_wls(1)
+        quantise_wls(2)
+        nc.vector.tensor_scalar_mul(out=half_bls[:], in0=bt_ps[:, 0:T4], scalar1=0.5)
+        quantise_wls(3)
+        nc.vector.tensor_copy(out=c_bc[:], in_=c_ps[:])
+        nc.vector.tensor_copy(out=bls_bc[:], in_=l_ps[:])
+
+        state = {}
+
+        def ls_stage(g):
+            accs = []
+            if MODES[g] == "H":
+                for j in range(T4):
+                    acc = bank("A" + str(j), [P, 512])
+                    mx(acc[:], wls_q[j], P, 0, hq[g], 512, 0, 512)
+                    accs.append(acc)
+            else:
+                for i in range(T4):
+                    acc = bank("A" + str(i), [P, XO])
+                    for r in range(T4):
+                        mx(acc[:, r * P : (r + 1) * P], hq[g], 512, i * P, wls_q[r], P, 0, P)
+                    accs.append(acc)
+            state["ls"] = accs
+
+        def t_stage(g):
+            ts = []
+            for i in range(T4):
+                t = etp.tile([P, XO], F32, tag="t", name="t")
+                nc.vector.tensor_tensor(out=t[:], in0=state["ls"][i][:], in1=bls_bc[:], op=ALU.add)
+                ts.append(t)
+            state["t"] = ts
+
+        def exp_stage(g):
             ets = []
             for j in range(T4):
                 et = etp.tile([P, 512], F32, tag="et", name="et")
-                nc.scalar.activation(
-                    out=et[:], in_=ls_banks[j][:], func=ACT.Exp, bias=half_bls[:, j : j + 1], scale=0.5
-                )
+                if MODES[g] == "H":
+                    nc.scalar.activation(
+                        out=et[:], in_=state["ls"][j][:], func=ACT.Exp, bias=half_bls[:, j : j + 1], scale=0.5
+                    )
+                else:
+                    nc.scalar.activation(out=et[:], in_=state["t"][j][:], func=ACT.Exp, scale=0.5)
                 ets.append(et)
-            u = upp.tile([P, T4 * XO], F32, tag="u", name="u")
+            state["et"] = ets
+
+        def mu_stage(g):
+            accs = []
             for i in range(T4):
                 acc = bank("B" + str(i), [P, XO])
-                mx(acc[:], hq[g], i * P, wmu_q, 0, XO)
-                nc.vector.tensor_tensor(out=u[:, i * XO : (i + 1) * XO], in0=acc[:], in1=c_bc[:], op=ALU.add)
-            prod = upp.tile([P, T4 * XO], F32, tag="prod", name="prod")
-            res = outp.tile([P, T4 * XO], F32, tag="res", name="res")
-            u3 = u[:].rearrange("p (i n) -> p i n", i=T4)
-            p3 = prod[:].rearrange("p (i n) -> p i n", i=T4)
-            r3 = res[:].rearrange("p (i n) -> p i n", i=T4)
-            e3 = eps_sb[g][:].rearrange("p (i n) -> p i n", i=T4)
+                mx(acc[:], hq[g], 512, i * P, wmu_q, 512, 0, XO)
+                accs.append(acc)
+            state["mu"] = accs
+
+        def u_stage(g):
+            u = upp.tile([P, T4 * XO], F32, tag="u", name="u")
+            for i in range(T4):
+                nc.vector.tensor_tensor(out=u[:, i * XO : (i + 1) * XO], in0=state["mu"][i][:], in1=c_bc[:], op=ALU.add)
+            state["u"] = u
+
+        def etr_stage(g):
+            ebs = []
             for j in range(T4):
                 eb = bank("A" + str(j), [P, T4, P])
                 for i in range(T4):
-                    nc.tensor.transpose(eb[:, i, :], ets[j][:, i * P : (i + 1) * P], ident[:])
-                cols = slice(j * P, (j + 1) * P)
-                nc.vector.tensor_tensor(out=p3[:, :, cols], in0=eb[:], in1=e3[:, :, cols], op=ALU.mult)
-                nc.gpsimd.tensor_tensor(out=r3[:, :, cols], in0=u3[:, :, cols], in1=p3[:, :, cols], op=ALU.add)
-            nc.sync.dma_start(out=out_v[g], in_=res[:])
+                    nc.tensor.transpose(eb[:, i, :], state["et"][j][:, i * P : (i + 1) * P], ident[:])
+                ebs.append(eb)
+            state["eb"] = ebs
+
+        def new_prod():
+            state["prod"] = upp.tile([P, T4 * XO], F32, tag="prod", name="prod")
+
+        def prod_h(g, j):
+            p3 = state["prod"][:].rearrange("p (i n) -> p i n", i=T4)
+            e3 = eps_sb[g][:].rearrange("p (i n) -> p i n", i=T4)
+            cols = slice(j * P, (j + 1) * P)
+            nc.vector.tensor_tensor(out=p3[:, :, cols], in0=state["eb"][j][:], in1=e3[:, :, cols], op=ALU.mult)
+
+        def prod_a(g, i):
+            cols = slice(i * XO, (i + 1) * XO)
+            eng = nc.vector if i < PROD_ON_V else nc.gpsimd
+            eng.tensor_tensor(out=state["prod"][:, cols], in0=state["et"][i][:], in1=eps_sb[g][:, cols], op=ALU.mult)
+
+        def finish(g):
+            res = outp.tile([P, T4 * XO], F32, tag="res", name="res")
+            u, prod = state["u"], state["prod"]
+            if MODES[g] == "H":
+                u3 = u[:].rearrange("p (i n) -> p i n", i=T4)
+                p3 = prod[:].rearrange("p (i n) -> p i n", i=T4)
+                r3 = res[:].rearrange("p (i n) -> p i n", i=T4)
+                last = g == GROUPS - 1
+                for j in range(T4):
+                    cols = slice(j * P, (j + 1) * P)
+                    eng = nc.vector if (last and j >= 2) else nc.gpsimd
+                    eng.tensor_tensor(out=r3[:, :, cols], in0=u3[:, :, cols], in1=p3[:, :, cols], op=ALU.add)
+                    if last and j % 2 == 1:
+                        half = slice((j - 1) * P, (j + 1) * P)
+                        nc.sync.dma_start(out=out_v3[g][:, :, half], in_=r3[:, :, half])
+                if not last:
+                    nc.sync.dma_start(out=out_v[g], in_=res[:])
+            else:
+                for i in range(T4):
+                    cols = slice(i * XO, (i + 1) * XO)
+                    nc.gpsimd.tensor_tensor(out=res[:, cols], in0=u[:, cols], in1=prod[:, cols], op=ALU.add)
+                nc.sync.dma_start(out=out_v[g], in_=res[:])
+
+        def htr_stage(g):
+            state["pending"] = [transpose_tile(hd_sb[g], i, "B" + str(i)) for i in range(T4)]
+
+        def regroup_stage(engines):
+            grp = new_grp()
+            for i in range(T4):
+                copy_out(engines[i], grp_slot(grp, i), state["pending"][i])
+            return grp
+
+        ls_stage(0)
+        exp_stage(0)
+        grp_mu = new_grp()
+        for r in range(T4):
+            copy_out("vs"[r % 2], grp_slot(grp_mu, r), transpose_tile(wmu_sb, r, "B" + str(r)))
+        etr_stage(0)
+        new_prod()
+        prod_h(0, 0)
+        prod_h(0, 1)
+        wmu_q = quantise(grp_mu, const, "wmu")
+        prod_h(0, 2)
+        prod_h(0, 3)
+        htr_stage(1)
+        grp_next = regroup_stage("vsvs")
+        mu_stage(0)
+        hq[1] = quantise(grp_next, hcp, "h")
+        u_stage(0)
+        finish(0)
+        htr_stage(2)
+
+        for g in range(1, GROUPS):
+            if g + 1 < GROUPS:
+                grp_next = regroup_stage("ssss")
+            ls_stage(g)
+            if g + 1 < GROUPS:
+                hq[g + 1] = quantise(grp_next, hcp, "h")
+            if MODES[g] == "A":
+                t_stage(g)
+            exp_stage(g)
+            mu_stage(g)
+            u_stage(g)
+            new_prod()
+            if MODES[g] == "H":
+                etr_stage(g)
+                for j in range(T4):
+                    prod_h(g, j)
+            else:
+                for i in range(T4):
+                    prod_a(g, i)
+            finish(g)
             if g + 2 < GROUPS:
-                pending = transposes(hd_sb[g + 2], "B")
+                htr_stage(g + 2)

@@ -17,7 +17,7 @@ T4 = 4
 GROUPS = B // (P * T4)
 PASSES = K // 512
 FLOPS = 2 * B * K * 2 * XO
-MODES = "HHHHHHHH"
+MODES = "HAHAHAHH"
 PROD_ON_V = 2
 
 

@@ -17,7 +17,8 @@ T4 = 4
 GROUPS = B // (P * T4)
 PASSES = K // 512
 FLOPS = 2 * B * K * 2 * XO
-MODES = "HAHAHAHH"
+MODES = "HHHHHHHH"
+G_COLS = 256
 PROD_ON_V = 2
 
 
@@ -267,13 +268,10 @@ def tile_vae_pb_t_kernel(tc, hd, W_mu_d, b_mu_d, W_ls_d, b_ls_d, eps_x, out):
                 p3 = prod[:].rearrange("p (i n) -> p i n", i=T4)
                 r3 = res[:].rearrange("p (i n) -> p i n", i=T4)
                 last = g == GROUPS - 1
-                for j in range(T4):
-                    cols = slice(j * P, (j + 1) * P)
-                    eng = nc.vector if (last and j >= 2) else nc.gpsimd
+                for eng, cols in ((nc.gpsimd, slice(0, G_COLS)), (nc.vector, slice(G_COLS, XO))):
                     eng.tensor_tensor(out=r3[:, :, cols], in0=u3[:, :, cols], in1=p3[:, :, cols], op=ALU.add)
-                    if last and j % 2 == 1:
-                        half = slice((j - 1) * P, (j + 1) * P)
-                        nc.sync.dma_start(out=out_v3[g][:, :, half], in_=r3[:, :, half])
+                    if last:
+                        nc.sync.dma_start(out=out_v3[g][:, :, cols], in_=r3[:, :, cols])
                 if not last:
                     nc.sync.dma_start(out=out_v[g], in_=res[:])
             else:

@@ -15,11 +15,10 @@ P = 128
 B, K, XO = 4096, 1024, 512
 T4 = 4
 GROUPS = B // (P * T4)
-PASSES = K // 512
+K_PASS = 512
+PASSES = K // K_PASS
+LAG = 2
 FLOPS = 2 * B * K * 2 * XO
-MODES = "HHHHHHHH"
-G_COLS = 256
-PROD_ON_V = 2
 
 
 def tile_vae_pb_t_kernel(tc, hd, W_mu_d, b_mu_d, W_ls_d, b_ls_d, eps_x, out):
@@ -28,7 +27,6 @@ def tile_vae_pb_t_kernel(tc, hd, W_mu_d, b_mu_d, W_ls_d, b_ls_d, eps_x, out):
     hd_pieces = hd.rearrange("(g p i) k -> g i p k", p=P, i=T4)
     eps_v = eps_x.rearrange("(g p i) n -> g p (i n)", p=P, i=T4)
     out_v = out.rearrange("(g p i) n -> g p (i n)", p=P, i=T4)
-    out_v3 = out.rearrange("(g p i) n -> g p i n", p=P, i=T4)
 
     with ExitStack() as ctx:
         const = ctx.enter_context(tc.tile_pool(name="const", bufs=1))
@@ -36,10 +34,10 @@ def tile_vae_pb_t_kernel(tc, hd, W_mu_d, b_mu_d, W_ls_d, b_ls_d, eps_x, out):
         epsp = ctx.enter_context(tc.tile_pool(name="epsp", bufs=GROUPS))
         grpp = ctx.enter_context(tc.tile_pool(name="grpp", bufs=2))
         grpw = ctx.enter_context(tc.tile_pool(name="grpw", bufs=4))
-        hcp = ctx.enter_context(tc.tile_pool(name="hcp", bufs=3))
+        hcp = ctx.enter_context(tc.tile_pool(name="hcp", bufs=5))
         etp = ctx.enter_context(tc.tile_pool(name="etp", bufs=4))
-        upp = ctx.enter_context(tc.tile_pool(name="upp", bufs=2))
-        outp = ctx.enter_context(tc.tile_pool(name="outp", bufs=4))
+        prodp = ctx.enter_context(tc.tile_pool(name="prodp", bufs=4))
+        resp = ctx.enter_context(tc.tile_pool(name="resp", bufs=3))
         psum = ctx.enter_context(tc.psum_pool(name="psum", bufs=1))
         ctx.enter_context(tc.manual_schedule())
 
@@ -52,8 +50,6 @@ def tile_vae_pb_t_kernel(tc, hd, W_mu_d, b_mu_d, W_ls_d, b_ls_d, eps_x, out):
         make_identity(nc, ident_bf[:])
         brow_mu = const.tile([P, XO], BF16, name="brow_mu")
         nc.vector.memset(brow_mu[:], 0.0)
-        brow_ls = const.tile([P, XO], BF16, name="brow_ls")
-        nc.vector.memset(brow_ls[:], 0.0)
         bcol = const.tile([P, P], BF16, name="bcol")
         nc.vector.memset(bcol[:], 0.0)
         ones = const.tile([P, P], BF16, name="ones")
@@ -62,12 +58,14 @@ def tile_vae_pb_t_kernel(tc, hd, W_mu_d, b_mu_d, W_ls_d, b_ls_d, eps_x, out):
         nc.vector.memset(warm[:], 0.0)
         nc.scalar.dma_start(out=bcol[0:T4, :], in_=b_ls_d.rearrange("(j q) -> j q", q=P))
         nc.scalar.dma_start(out=brow_mu[0:1, :], in_=b_mu_d.rearrange("(o n) -> o n", o=1))
-        nc.scalar.dma_start(out=brow_ls[0:1, :], in_=b_ls_d.rearrange("(o n) -> o n", o=1))
         warm2 = const.tile([P, 1], F32, name="warm2")
         nc.scalar.activation(out=warm2[:], in_=warm[:], func=ACT.Exp)
 
-        hd_sb = {}
-        eps_sb = {}
+        hd_sb, eps_sb, w_sb = {}, {}, {}
+        pend, grp, hq = {}, {}, {}
+        wpend, wls_grp, wq = {}, {}, {}
+        ls_ps, et_sb, e_ps, mu_ps, prod, res = {}, {}, {}, {}, {}, {}
+        small = {}
 
         def load_hd(g, pieces):
             t = raw.tile([P, T4 * K], BF16, tag="raw", name="hd_sb")
@@ -78,26 +76,16 @@ def tile_vae_pb_t_kernel(tc, hd, W_mu_d, b_mu_d, W_ls_d, b_ls_d, eps_x, out):
                 nc.sync.dma_start(out=t[:], in_=hd_v[g])
             hd_sb[g] = t
 
-        def load_w(w, nm):
+        def load_w(nm, w):
             t = const.tile([P, T4 * K], BF16, name=nm)
             for r in range(T4):
                 nc.sync.dma_start(out=t[:, r * K : (r + 1) * K], in_=w[r * P : (r + 1) * P, :])
-            return t
+            w_sb[nm] = t
 
         def load_eps(g):
             t = epsp.tile([P, T4 * XO], BF16, tag="eps", name="eps_sb")
             nc.sync.dma_start(out=t[:], in_=eps_v[g])
             eps_sb[g] = t
-
-        load_hd(0, True)
-        wls_sb = load_w(W_ls_d, "wls_sb")
-        wmu_sb = load_w(W_mu_d, "wmu_sb")
-        load_eps(0)
-        load_hd(1, False)
-        for g in range(2, GROUPS):
-            load_hd(g, False)
-            load_eps(g - 1)
-        load_eps(GROUPS - 1)
 
         def transpose_tile(src, i, tag):
             words = src[:].bitcast(F32)
@@ -109,225 +97,220 @@ def tile_vae_pb_t_kernel(tc, hd, W_mu_d, b_mu_d, W_ls_d, b_ls_d, eps_x, out):
 
         def copy_out(eng, dst, bk):
             src = bk[:].rearrange("p (g u) b -> p g b u", u=2)
-            if eng == "v":
+            if eng == "V":
                 nc.vector.tensor_copy(out=dst, in_=src)
             else:
                 nc.scalar.copy(out=dst, in_=src)
 
-        def new_grp():
-            return grpp.tile([P, T4 * K], BF16, tag="grp", name="grp", align_bytes=64)
-
-        def grp_slot(grp, i):
-            gw = grp[:].bitcast(F32).rearrange("p (g c u) -> p g c u", g=PASSES, u=2)
+        def group_slot(t, i):
+            gw = t[:].bitcast(F32).rearrange("p (g c u) -> p g c u", g=PASSES, u=2)
             return gw[:, :, i * P : (i + 1) * P, :]
 
-        def quantise(grp, pool, tag):
+        def quantise_group(t, pool, tag):
             codes = pool.tile([P, PASSES * 512], U32, tag=tag + "c", name=tag + "c", align_bytes=64)
             scales = pool.tile([P, PASSES * 512], U8, tag=tag + "s", name=tag + "s", align_bytes=64)
             for c in range(PASSES):
                 nc.vector.quantize_mx(
                     out=codes[:, c * 512 : (c + 1) * 512].bitcast(FP8X4),
                     scales=scales[:, c * 512 : (c + 1) * 512],
-                    in_=grp[:, c * 2048 : (c + 1) * 2048],
+                    in_=t[:, c * 2048 : (c + 1) * 2048],
                 )
             return codes, scales
 
-        def mx(acc, stat, s_pitch, s0, mov, m_pitch, m0, n):
+        def trh(g, i, tag):
+            pend[g, i] = transpose_tile(hd_sb[g], i, tag)
+
+        def cph(eng, g, i):
+            if g not in grp:
+                grp[g] = grpp.tile([P, T4 * K], BF16, tag="grp", name="grp", align_bytes=64)
+            copy_out(eng, group_slot(grp[g], i), pend[g, i])
+
+        def qh(g):
+            if g == "wmu":
+                hq[g] = quantise_group(grp[g], const, "wmu")
+            else:
+                hq[g] = quantise_group(grp[g], hcp, "h")
+
+        def trw(nm, r, tag):
+            wpend[nm, r] = transpose_tile(w_sb[nm], r, tag)
+
+        def cp_wls(r):
+            t = grpw.tile([P, K], BF16, tag="grpw", name="grpw", align_bytes=64)
+            copy_out("S", t[:].bitcast(F32).rearrange("p (g c u) -> p g c u", g=PASSES, u=2), wpend["wls", r])
+            wls_grp[r] = t
+
+        def q_wls(r):
+            codes = const.tile([P, PASSES * P], U32, name="wlsc" + str(r), align_bytes=64)
+            scales = const.tile([P, PASSES * P], U8, name="wlss" + str(r), align_bytes=64)
+            nc.vector.quantize_mx(out=codes[:].bitcast(FP8X4), scales=scales[:], in_=wls_grp[r][:])
+            wq[r] = (codes, scales)
+
+        def cp_wmu(eng, r):
+            cph(eng, "wmu", r)
+
+        def mx(acc, stat, s_pitch, s0, mov, m_pitch):
             for c in range(PASSES):
                 a = c * s_pitch + s0
-                b = c * m_pitch + m0
+                b = c * m_pitch
                 nc.tensor.matmul_mx(
                     out=acc,
                     lhsT=stat[0][:, a : a + P].bitcast(FP8X4),
                     lhsT_scale=stat[1][:, a : a + P],
-                    rhs=mov[0][:, b : b + n].bitcast(FP8X4),
-                    rhs_scale=mov[1][:, b : b + n],
+                    rhs=mov[0][:, b : b + 512].bitcast(FP8X4),
+                    rhs_scale=mov[1][:, b : b + 512],
                     start=(c == 0),
                     stop=(c == PASSES - 1),
                 )
 
-        hq = {}
-        wls_q = {}
+        def bias_t():
+            small["bt"] = bank("B0", [P, P], BF16)
+            nc.tensor.transpose(small["bt"][:], bcol[:], ident_bf[:])
+            small["c"] = bank("B1", [P, XO])
+            nc.tensor.matmul(out=small["c"][:], lhsT=ones[:], rhs=brow_mu[:], start=True, stop=True)
 
-        grp0 = new_grp()
-        for i in range(T4):
-            copy_out("vs"[i % 2], grp_slot(grp0, i), transpose_tile(hd_sb[0], i, "B" + str(i)))
-        hq[0] = quantise(grp0, hcp, "h")
-
-        wls_grp = []
-        for r in range(T4):
-            gt = grpw.tile([P, K], BF16, tag="grpw", name="grpw", align_bytes=64)
-            dst = gt[:].bitcast(F32).rearrange("p (g c u) -> p g c u", g=PASSES, u=2)
-            copy_out("s", dst, transpose_tile(wls_sb, r, "A" + str(r)))
-            wls_grp.append(gt)
-
-        bt_ps = bank("B0", [P, P], BF16)
-        nc.tensor.transpose(bt_ps[:], bcol[:], ident_bf[:])
-        c_ps = bank("B1", [P, XO])
-        nc.tensor.matmul(out=c_ps[:], lhsT=ones[:], rhs=brow_mu[:], start=True, stop=True)
-        l_ps = bank("B2", [P, XO])
-        nc.tensor.matmul(out=l_ps[:], lhsT=ones[:], rhs=brow_ls[:], start=True, stop=True)
         half_bls = const.tile([P, T4], F32, name="half_bls")
-        c_bc = const.tile([P, XO], F32, name="c_bc")
-        bls_bc = const.tile([P, XO], F32, name="bls_bc")
+        c4 = const.tile([P, T4 * XO], F32, name="c4")
 
-        def quantise_wls(r):
-            codes = const.tile([P, PASSES * P], U32, name="wlsc" + str(r), align_bytes=64)
-            scales = const.tile([P, PASSES * P], U8, name="wlss" + str(r), align_bytes=64)
-            nc.vector.quantize_mx(out=codes[:].bitcast(FP8X4), scales=scales[:], in_=wls_grp[r][:])
-            wls_q[r] = (codes, scales)
+        def bias_half():
+            nc.vector.tensor_scalar_mul(out=half_bls[:], in0=small["bt"][:, 0:T4], scalar1=0.5)
 
-        quantise_wls(0)
-        quantise_wls(1)
-        quantise_wls(2)
-        nc.vector.tensor_scalar_mul(out=half_bls[:], in0=bt_ps[:, 0:T4], scalar1=0.5)
-        quantise_wls(3)
-        nc.vector.tensor_copy(out=c_bc[:], in_=c_ps[:])
-        nc.vector.tensor_copy(out=bls_bc[:], in_=l_ps[:])
-
-        state = {}
-
-        def ls_stage(g):
-            accs = []
-            if MODES[g] == "H":
-                for j in range(T4):
-                    acc = bank("A" + str(j), [P, 512])
-                    mx(acc[:], wls_q[j], P, 0, hq[g], 512, 0, 512)
-                    accs.append(acc)
-            else:
-                for i in range(T4):
-                    acc = bank("A" + str(i), [P, XO])
-                    for r in range(T4):
-                        mx(acc[:, r * P : (r + 1) * P], hq[g], 512, i * P, wls_q[r], P, 0, P)
-                    accs.append(acc)
-            state["ls"] = accs
-
-        def t_stage(g):
-            ts = []
+        def bias_c4():
             for i in range(T4):
-                t = etp.tile([P, XO], F32, tag="t", name="t")
-                nc.vector.tensor_tensor(out=t[:], in0=state["ls"][i][:], in1=bls_bc[:], op=ALU.add)
-                ts.append(t)
-            state["t"] = ts
+                nc.vector.tensor_copy(out=c4[:, i * XO : (i + 1) * XO], in_=small["c"][:])
 
-        def exp_stage(g):
-            ets = []
-            for j in range(T4):
-                et = etp.tile([P, 512], F32, tag="et", name="et")
-                if MODES[g] == "H":
-                    nc.scalar.activation(
-                        out=et[:], in_=state["ls"][j][:], func=ACT.Exp, bias=half_bls[:, j : j + 1], scale=0.5
-                    )
-                else:
-                    nc.scalar.activation(out=et[:], in_=state["t"][j][:], func=ACT.Exp, scale=0.5)
-                ets.append(et)
-            state["et"] = ets
+        def ls(g, j):
+            ls_ps[g, j] = bank("A" + str(j), [P, 512])
+            mx(ls_ps[g, j][:], wq[j], P, 0, hq[g], 512)
 
-        def mu_stage(g):
-            accs = []
+        def ex(g, j):
+            et_sb[g, j] = etp.tile([P, 512], F32, tag="et", name="et")
+            nc.scalar.activation(
+                out=et_sb[g, j][:], in_=ls_ps[g, j][:], func=ACT.Exp, bias=half_bls[:, j : j + 1], scale=0.5
+            )
+
+        def etr(g, j):
+            e_ps[g, j] = bank("A" + str(j), [P, T4, P])
             for i in range(T4):
-                acc = bank("B" + str(i), [P, XO])
-                mx(acc[:], hq[g], 512, i * P, wmu_q, 512, 0, XO)
-                accs.append(acc)
-            state["mu"] = accs
+                nc.tensor.transpose(e_ps[g, j][:, i, :], et_sb[g, j][:, i * P : (i + 1) * P], ident[:])
 
-        def u_stage(g):
-            u = upp.tile([P, T4 * XO], F32, tag="u", name="u")
-            for i in range(T4):
-                nc.vector.tensor_tensor(out=u[:, i * XO : (i + 1) * XO], in0=state["mu"][i][:], in1=c_bc[:], op=ALU.add)
-            state["u"] = u
+        def by_tile(t):
+            return t[:].rearrange("p (i n) -> p i n", i=T4)
 
-        def etr_stage(g):
-            ebs = []
-            for j in range(T4):
-                eb = bank("A" + str(j), [P, T4, P])
-                for i in range(T4):
-                    nc.tensor.transpose(eb[:, i, :], state["et"][j][:, i * P : (i + 1) * P], ident[:])
-                ebs.append(eb)
-            state["eb"] = ebs
-
-        def new_prod():
-            state["prod"] = upp.tile([P, T4 * XO], F32, tag="prod", name="prod")
-
-        def prod_h(g, j):
-            p3 = state["prod"][:].rearrange("p (i n) -> p i n", i=T4)
-            e3 = eps_sb[g][:].rearrange("p (i n) -> p i n", i=T4)
+        def ph(g, j):
+            if g not in prod:
+                prod[g] = prodp.tile([P, T4 * XO], F32, tag="prod", name="prod")
             cols = slice(j * P, (j + 1) * P)
-            nc.vector.tensor_tensor(out=p3[:, :, cols], in0=state["eb"][j][:], in1=e3[:, :, cols], op=ALU.mult)
+            nc.vector.tensor_tensor(
+                out=by_tile(prod[g])[:, :, cols], in0=e_ps[g, j][:], in1=by_tile(eps_sb[g])[:, :, cols], op=ALU.mult
+            )
 
-        def prod_a(g, i):
+        def pc(g, j):
+            cols = slice(j * P, (j + 1) * P)
+            nc.gpsimd.tensor_tensor(
+                out=by_tile(prod[g])[:, :, cols], in0=by_tile(prod[g])[:, :, cols], in1=by_tile(c4)[:, :, cols], op=ALU.add
+            )
+
+        def mu(g, i):
+            mu_ps[g, i] = bank("B" + str(i), [P, XO])
+            mx(mu_ps[g, i][:], hq[g], 512, i * P, hq["wmu"], 512)
+
+        def rs(g, i):
+            if g not in res:
+                res[g] = resp.tile([P, T4 * XO], F32, tag="res", name="res")
             cols = slice(i * XO, (i + 1) * XO)
-            eng = nc.vector if i < PROD_ON_V else nc.gpsimd
-            eng.tensor_tensor(out=state["prod"][:, cols], in0=state["et"][i][:], in1=eps_sb[g][:, cols], op=ALU.mult)
+            nc.vector.tensor_tensor(out=res[g][:, cols], in0=mu_ps[g, i][:], in1=prod[g][:, cols], op=ALU.add)
 
-        def finish(g):
-            res = outp.tile([P, T4 * XO], F32, tag="res", name="res")
-            u, prod = state["u"], state["prod"]
-            if MODES[g] == "H":
-                u3 = u[:].rearrange("p (i n) -> p i n", i=T4)
-                p3 = prod[:].rearrange("p (i n) -> p i n", i=T4)
-                r3 = res[:].rearrange("p (i n) -> p i n", i=T4)
-                last = g == GROUPS - 1
-                for eng, cols in ((nc.gpsimd, slice(0, G_COLS)), (nc.vector, slice(G_COLS, XO))):
-                    eng.tensor_tensor(out=r3[:, :, cols], in0=u3[:, :, cols], in1=p3[:, :, cols], op=ALU.add)
-                    if last:
-                        nc.sync.dma_start(out=out_v3[g][:, :, cols], in_=r3[:, :, cols])
-                if not last:
-                    nc.sync.dma_start(out=out_v[g], in_=res[:])
-            else:
-                for i in range(T4):
-                    cols = slice(i * XO, (i + 1) * XO)
-                    nc.gpsimd.tensor_tensor(out=res[:, cols], in0=u[:, cols], in1=prod[:, cols], op=ALU.add)
-                nc.sync.dma_start(out=out_v[g], in_=res[:])
+        def store(g, i0, i1):
+            cols = slice(i0 * XO, i1 * XO)
+            nc.sync.dma_start(out=out_v[g][:, cols], in_=res[g][:, cols])
 
-        def htr_stage(g):
-            state["pending"] = [transpose_tile(hd_sb[g], i, "B" + str(i)) for i in range(T4)]
+        R4 = range(T4)
+        load_hd(0, True)
+        load_w("wls", W_ls_d)
+        load_hd(1, True)
+        load_eps(0)
+        load_hd(2, False)
+        load_w("wmu", W_mu_d)
+        load_eps(1)
+        for g in range(3, GROUPS):
+            load_hd(g, False)
+            load_eps(g - 1)
+        load_eps(GROUPS - 1)
 
-        def regroup_stage(engines):
-            grp = new_grp()
-            for i in range(T4):
-                copy_out(engines[i], grp_slot(grp, i), state["pending"][i])
-            return grp
-
-        ls_stage(0)
-        exp_stage(0)
-        grp_mu = new_grp()
-        for r in range(T4):
-            copy_out("vs"[r % 2], grp_slot(grp_mu, r), transpose_tile(wmu_sb, r, "B" + str(r)))
-        etr_stage(0)
-        new_prod()
-        prod_h(0, 0)
-        prod_h(0, 1)
-        wmu_q = quantise(grp_mu, const, "wmu")
-        prod_h(0, 2)
-        prod_h(0, 3)
-        htr_stage(1)
-        grp_next = regroup_stage("vsvs")
-        mu_stage(0)
-        hq[1] = quantise(grp_next, hcp, "h")
-        u_stage(0)
-        finish(0)
-        htr_stage(2)
-
-        for g in range(1, GROUPS):
+        for i in R4:
+            trh(0, i, "B" + str(i))
+            cph("VS"[i % 2], 0, i)
+        qh(0)
+        for r in R4:
+            trw("wls", r, "A" + str(r))
+            cp_wls(r)
+        q_wls(0)
+        q_wls(1)
+        q_wls(2)
+        bias_t()
+        bias_half()
+        q_wls(3)
+        for j in R4:
+            ls(0, j)
+        for j in R4:
+            ex(0, j)
+        bias_c4()
+        hb = ("B2", "B3", "B0", "B1")
+        for i in R4:
+            trh(1, i, hb[i])
+            cph("VS"[i % 2], 1, i)
+        qh(1)
+        for j in R4:
+            etr(0, j)
+        for j in R4:
+            ph(0, j)
+            pc(0, j)
+        for i in R4:
+            trh(2, i, hb[i])
+        for i in R4:
+            cph("S", 2, i)
+        for j in R4:
+            ls(1, j)
+        qh(2)
+        for j in R4:
+            ex(1, j)
+        for r in R4:
+            pend["wmu", r] = transpose_tile(w_sb["wmu"], r, hb[r])
+            cp_wmu("VS"[r % 2], r)
+        for j in R4:
+            etr(1, j)
+        for j in R4:
+            ph(1, j)
+            pc(1, j)
+        qh("wmu")
+        for i in R4:
+            trh(3, i, hb[i])
+        for g in range(LAG, GROUPS):
             if g + 1 < GROUPS:
-                grp_next = regroup_stage("ssss")
-            ls_stage(g)
+                for i in R4:
+                    cph("S", g + 1, i)
+            for j in R4:
+                ls(g, j)
             if g + 1 < GROUPS:
-                hq[g + 1] = quantise(grp_next, hcp, "h")
-            if MODES[g] == "A":
-                t_stage(g)
-            exp_stage(g)
-            mu_stage(g)
-            u_stage(g)
-            new_prod()
-            if MODES[g] == "H":
-                etr_stage(g)
-                for j in range(T4):
-                    prod_h(g, j)
-            else:
-                for i in range(T4):
-                    prod_a(g, i)
-            finish(g)
+                qh(g + 1)
+            for j in R4:
+                ex(g, j)
+            for i in R4:
+                mu(g - LAG, i)
+            for i in R4:
+                rs(g - LAG, i)
+            store(g - LAG, 0, T4)
+            for j in R4:
+                etr(g, j)
+            for j in R4:
+                ph(g, j)
+                pc(g, j)
             if g + 2 < GROUPS:
-                htr_stage(g + 2)
+                for i in R4:
+                    trh(g + 2, i, "B" + str(i))
+        for g in range(GROUPS - LAG, GROUPS):
+            for i in R4:
+                mu(g, i)
+            for i in R4:
+                rs(g, i)
+                store(g, i, i + 1)

@@ -285,6 +285,23 @@ def tile_vae_pb_t_kernel(tc, hd, W_mu_d, b_mu_d, W_ls_d, b_ls_d, eps_x, out):
         qh("wmu")
         for i in R4:
             trh(3, i, hb[i])
+        def mu_group(g, fine):
+            for i in R4:
+                mu(g, i)
+            for i in R4:
+                rs(g, i)
+                if fine:
+                    store(g, i, i + 1)
+            if not fine:
+                store(g, 0, T4)
+
+        def exp_back(g):
+            for j in R4:
+                etr(g, j)
+            for j in R4:
+                ph(g, j)
+                pc(g, j)
+
         for g in range(LAG, GROUPS):
             if g + 1 < GROUPS:
                 for i in R4:
@@ -295,22 +312,13 @@ def tile_vae_pb_t_kernel(tc, hd, W_mu_d, b_mu_d, W_ls_d, b_ls_d, eps_x, out):
                 qh(g + 1)
             for j in R4:
                 ex(g, j)
-            for i in R4:
-                mu(g - LAG, i)
-            for i in R4:
-                rs(g - LAG, i)
-            store(g - LAG, 0, T4)
-            for j in R4:
-                etr(g, j)
-            for j in R4:
-                ph(g, j)
-                pc(g, j)
             if g + 2 < GROUPS:
+                mu_group(g - LAG, False)
+                exp_back(g)
                 for i in R4:
                     trh(g + 2, i, "B" + str(i))
+            else:
+                exp_back(g)
+                mu_group(g - LAG, g == GROUPS - 1)
         for g in range(GROUPS - LAG, GROUPS):
-            for i in R4:
-                mu(g, i)
-            for i in R4:
-                rs(g, i)
-                store(g, i, i + 1)
+            mu_group(g, True)

@@ -13,31 +13,42 @@ ALU = mybir.AluOpType
 
 P = 128
 B, K, XO = 4096, 1024, 512
-T4 = 4
-GROUPS = B // (P * T4)
+MOVING = 512
+GROUP = MOVING
+GROUPS = B // GROUP
+ROW_TILES = GROUP // P
+OUT_TILES = XO // P
+PACK = 4
 K_PASS = 512
 PASSES = K // K_PASS
+WORDS = K // 2
+PLANES = WORDS // P
 LAG = 2
 FLOPS = 2 * B * K * 2 * XO
+
+assert XO == MOVING
+assert OUT_TILES == ROW_TILES
 
 
 def tile_vae_pb_t_kernel(tc, hd, W_mu_d, b_mu_d, W_ls_d, b_ls_d, eps_x, out):
     nc = tc.nc
-    hd_v = hd.rearrange("(g p i) k -> g p (i k)", p=P, i=T4)
-    hd_pieces = hd.rearrange("(g p i) k -> g i p k", p=P, i=T4)
-    eps_v = eps_x.rearrange("(g p i) n -> g p (i n)", p=P, i=T4)
-    out_v = out.rearrange("(g p i) n -> g p (i n)", p=P, i=T4)
+    hd_groups = hd.rearrange("(g p i) k -> g p (i k)", p=P, i=ROW_TILES)
+    hd_tiles = hd.rearrange("(g p i) k -> g i p k", p=P, i=ROW_TILES)
+    eps_groups = eps_x.rearrange("(g p i) n -> g p (i n)", p=P, i=ROW_TILES)
+    out_groups = out.rearrange("(g p i) n -> g p (i n)", p=P, i=ROW_TILES)
+    row_tiles = range(ROW_TILES)
+    out_tiles = range(OUT_TILES)
 
     with ExitStack() as ctx:
         const = ctx.enter_context(tc.tile_pool(name="const", bufs=1))
         raw = ctx.enter_context(tc.tile_pool(name="raw", bufs=4))
-        epsp = ctx.enter_context(tc.tile_pool(name="epsp", bufs=GROUPS))
-        grpp = ctx.enter_context(tc.tile_pool(name="grpp", bufs=2))
-        grpw = ctx.enter_context(tc.tile_pool(name="grpw", bufs=4))
-        hcp = ctx.enter_context(tc.tile_pool(name="hcp", bufs=5))
-        etp = ctx.enter_context(tc.tile_pool(name="etp", bufs=4))
-        prodp = ctx.enter_context(tc.tile_pool(name="prodp", bufs=4))
-        resp = ctx.enter_context(tc.tile_pool(name="resp", bufs=3))
+        eps_pool = ctx.enter_context(tc.tile_pool(name="eps", bufs=GROUPS))
+        qin_pool = ctx.enter_context(tc.tile_pool(name="quant_in", bufs=2))
+        wls_pool = ctx.enter_context(tc.tile_pool(name="wls_in", bufs=OUT_TILES))
+        code_pool = ctx.enter_context(tc.tile_pool(name="hd_codes", bufs=5))
+        exp_pool = ctx.enter_context(tc.tile_pool(name="exp_t", bufs=OUT_TILES))
+        prod_pool = ctx.enter_context(tc.tile_pool(name="prod", bufs=4))
+        res_pool = ctx.enter_context(tc.tile_pool(name="res", bufs=3))
         psum = ctx.enter_context(tc.psum_pool(name="psum", bufs=1))
         ctx.enter_context(tc.manual_schedule())
 
@@ -56,175 +67,176 @@ def tile_vae_pb_t_kernel(tc, hd, W_mu_d, b_mu_d, W_ls_d, b_ls_d, eps_x, out):
         nc.vector.memset(ones[:], 1.0)
         warm = const.tile([P, 1], F32, name="warm")
         nc.vector.memset(warm[:], 0.0)
-        nc.scalar.dma_start(out=bcol[0:T4, :], in_=b_ls_d.rearrange("(j q) -> j q", q=P))
+        nc.scalar.dma_start(out=bcol[0:OUT_TILES, :], in_=b_ls_d.rearrange("(j q) -> j q", q=P))
         nc.scalar.dma_start(out=brow_mu[0:1, :], in_=b_mu_d.rearrange("(o n) -> o n", o=1))
         warm2 = const.tile([P, 1], F32, name="warm2")
         nc.scalar.activation(out=warm2[:], in_=warm[:], func=ACT.Exp)
 
-        hd_sb, eps_sb, w_sb = {}, {}, {}
-        pend, grp, hq = {}, {}, {}
-        wpend, wls_grp, wq = {}, {}, {}
-        ls_ps, et_sb, e_ps, mu_ps, prod, res = {}, {}, {}, {}, {}, {}
-        small = {}
+        loaded, eps_sb = {}, {}
+        flipped = {}
+        quant_in, quantised = {}, {}
+        wls_in, wls_q = {}, {}
+        ls_ps, exp_t, exp_ps, mu_ps, prod, res = {}, {}, {}, {}, {}, {}
+        bias_ps = {}
 
-        def load_hd(g, pieces):
-            t = raw.tile([P, T4 * K], BF16, tag="raw", name="hd_sb")
-            if pieces:
-                for i in range(T4):
-                    nc.sync.dma_start(out=t[:, i * K : (i + 1) * K], in_=hd_pieces[g, i])
+        def load_hd(g, in_tiles):
+            t = raw.tile([P, ROW_TILES * K], BF16, tag="raw", name="hd_sb")
+            if in_tiles:
+                for i in row_tiles:
+                    nc.sync.dma_start(out=t[:, i * K : (i + 1) * K], in_=hd_tiles[g, i])
             else:
-                nc.sync.dma_start(out=t[:], in_=hd_v[g])
-            hd_sb[g] = t
+                nc.sync.dma_start(out=t[:], in_=hd_groups[g])
+            loaded[g] = t
 
-        def load_w(nm, w):
-            t = const.tile([P, T4 * K], BF16, name=nm)
-            for r in range(T4):
+        def load_w(name, w):
+            t = const.tile([P, OUT_TILES * K], BF16, name=name)
+            for r in out_tiles:
                 nc.sync.dma_start(out=t[:, r * K : (r + 1) * K], in_=w[r * P : (r + 1) * P, :])
-            w_sb[nm] = t
+            loaded[name] = t
 
         def load_eps(g):
-            t = epsp.tile([P, T4 * XO], BF16, tag="eps", name="eps_sb")
-            nc.sync.dma_start(out=t[:], in_=eps_v[g])
+            t = eps_pool.tile([P, ROW_TILES * XO], BF16, tag="eps", name="eps_sb")
+            nc.sync.dma_start(out=t[:], in_=eps_groups[g])
             eps_sb[g] = t
 
-        def transpose_tile(src, i, tag):
-            words = src[:].bitcast(F32)
-            bk = bank(tag, [P, 4, P])
-            for s in range(4):
-                c0 = i * 512 + s * P
+        def flip(g, i, tag):
+            words = loaded[g][:].bitcast(F32)
+            bk = bank(tag, [P, PLANES, P])
+            for s in range(PLANES):
+                c0 = i * WORDS + s * P
                 nc.tensor.transpose(bk[:, s, :], words[:, c0 : c0 + P], ident[:])
-            return bk
+            flipped[g, i] = bk
 
-        def copy_out(eng, dst, bk):
-            src = bk[:].rearrange("p (g u) b -> p g b u", u=2)
-            if eng == "V":
+        def copy_out(engine, dst, bk):
+            src = bk[:].rearrange("p (c u) n -> p c n u", u=2)
+            if engine == "V":
                 nc.vector.tensor_copy(out=dst, in_=src)
             else:
                 nc.scalar.copy(out=dst, in_=src)
 
-        def group_slot(t, i):
-            gw = t[:].bitcast(F32).rearrange("p (g c u) -> p g c u", g=PASSES, u=2)
-            return gw[:, :, i * P : (i + 1) * P, :]
+        def as_words(t):
+            return t[:].bitcast(F32).rearrange("p (c n u) -> p c n u", c=PASSES, u=2)
 
-        def quantise_group(t, pool, tag):
-            codes = pool.tile([P, PASSES * 512], U32, tag=tag + "c", name=tag + "c", align_bytes=64)
-            scales = pool.tile([P, PASSES * 512], U8, tag=tag + "s", name=tag + "s", align_bytes=64)
+        def regroup(engine, g, i):
+            if g not in quant_in:
+                quant_in[g] = qin_pool.tile([P, ROW_TILES * K], BF16, tag="quant_in", name="quant_in", align_bytes=64)
+            copy_out(engine, as_words(quant_in[g])[:, :, i * P : (i + 1) * P, :], flipped[g, i])
+
+        def quantise(g):
+            pool, tag = (const, "wmu") if g == "wmu" else (code_pool, "hd")
+            codes = pool.tile([P, PASSES * MOVING], U32, tag=tag + "c", name=tag + "c", align_bytes=64)
+            scales = pool.tile([P, PASSES * MOVING], U8, tag=tag + "s", name=tag + "s", align_bytes=64)
             for c in range(PASSES):
                 nc.vector.quantize_mx(
-                    out=codes[:, c * 512 : (c + 1) * 512].bitcast(FP8X4),
-                    scales=scales[:, c * 512 : (c + 1) * 512],
-                    in_=t[:, c * 2048 : (c + 1) * 2048],
+                    out=codes[:, c * MOVING : (c + 1) * MOVING].bitcast(FP8X4),
+                    scales=scales[:, c * MOVING : (c + 1) * MOVING],
+                    in_=quant_in[g][:, c * PACK * MOVING : (c + 1) * PACK * MOVING],
                 )
-            return codes, scales
+            quantised[g] = (codes, scales)
 
-        def trh(g, i, tag):
-            pend[g, i] = transpose_tile(hd_sb[g], i, tag)
+        def regroup_wls(r):
+            t = wls_pool.tile([P, K], BF16, tag="wls_in", name="wls_in", align_bytes=64)
+            copy_out("S", as_words(t), flipped["wls", r])
+            wls_in[r] = t
 
-        def cph(eng, g, i):
-            if g not in grp:
-                grp[g] = grpp.tile([P, T4 * K], BF16, tag="grp", name="grp", align_bytes=64)
-            copy_out(eng, group_slot(grp[g], i), pend[g, i])
-
-        def qh(g):
-            if g == "wmu":
-                hq[g] = quantise_group(grp[g], const, "wmu")
-            else:
-                hq[g] = quantise_group(grp[g], hcp, "h")
-
-        def trw(nm, r, tag):
-            wpend[nm, r] = transpose_tile(w_sb[nm], r, tag)
-
-        def cp_wls(r):
-            t = grpw.tile([P, K], BF16, tag="grpw", name="grpw", align_bytes=64)
-            copy_out("S", t[:].bitcast(F32).rearrange("p (g c u) -> p g c u", g=PASSES, u=2), wpend["wls", r])
-            wls_grp[r] = t
-
-        def q_wls(r):
+        def quantise_wls(r):
             codes = const.tile([P, PASSES * P], U32, name="wlsc" + str(r), align_bytes=64)
             scales = const.tile([P, PASSES * P], U8, name="wlss" + str(r), align_bytes=64)
-            nc.vector.quantize_mx(out=codes[:].bitcast(FP8X4), scales=scales[:], in_=wls_grp[r][:])
-            wq[r] = (codes, scales)
+            nc.vector.quantize_mx(out=codes[:].bitcast(FP8X4), scales=scales[:], in_=wls_in[r][:])
+            wls_q[r] = (codes, scales)
 
-        def cp_wmu(eng, r):
-            cph(eng, "wmu", r)
-
-        def mx(acc, stat, s_pitch, s0, mov, m_pitch):
+        def mx_group(acc, stationary, pitch, first, moving):
             for c in range(PASSES):
-                a = c * s_pitch + s0
-                b = c * m_pitch
+                a = c * pitch + first
+                b = c * MOVING
                 nc.tensor.matmul_mx(
                     out=acc,
-                    lhsT=stat[0][:, a : a + P].bitcast(FP8X4),
-                    lhsT_scale=stat[1][:, a : a + P],
-                    rhs=mov[0][:, b : b + 512].bitcast(FP8X4),
-                    rhs_scale=mov[1][:, b : b + 512],
+                    lhsT=stationary[0][:, a : a + P].bitcast(FP8X4),
+                    lhsT_scale=stationary[1][:, a : a + P],
+                    rhs=moving[0][:, b : b + MOVING].bitcast(FP8X4),
+                    rhs_scale=moving[1][:, b : b + MOVING],
                     start=(c == 0),
                     stop=(c == PASSES - 1),
                 )
 
-        def bias_t():
-            small["bt"] = bank("B0", [P, P], BF16)
-            nc.tensor.transpose(small["bt"][:], bcol[:], ident_bf[:])
-            small["c"] = bank("B1", [P, XO])
-            nc.tensor.matmul(out=small["c"][:], lhsT=ones[:], rhs=brow_mu[:], start=True, stop=True)
+        def spread_biases():
+            bias_ps["ls"] = bank("B0", [P, P], BF16)
+            nc.tensor.transpose(bias_ps["ls"][:], bcol[:], ident_bf[:])
+            bias_ps["mu"] = bank("B1", [P, XO])
+            nc.tensor.matmul(out=bias_ps["mu"][:], lhsT=ones[:], rhs=brow_mu[:], start=True, stop=True)
 
-        half_bls = const.tile([P, T4], F32, name="half_bls")
-        c4 = const.tile([P, T4 * XO], F32, name="c4")
+        half_bls = const.tile([P, OUT_TILES], F32, name="half_bls")
+        bmu_rows = const.tile([P, ROW_TILES * XO], F32, name="bmu_rows")
 
-        def bias_half():
-            nc.vector.tensor_scalar_mul(out=half_bls[:], in0=small["bt"][:, 0:T4], scalar1=0.5)
+        def keep_half_bls():
+            nc.vector.tensor_scalar_mul(out=half_bls[:], in0=bias_ps["ls"][:, 0:OUT_TILES], scalar1=0.5)
 
-        def bias_c4():
-            for i in range(T4):
-                nc.vector.tensor_copy(out=c4[:, i * XO : (i + 1) * XO], in_=small["c"][:])
+        def keep_bmu():
+            for i in row_tiles:
+                nc.vector.tensor_copy(out=bmu_rows[:, i * XO : (i + 1) * XO], in_=bias_ps["mu"][:])
 
-        def ls(g, j):
-            ls_ps[g, j] = bank("A" + str(j), [P, 512])
-            mx(ls_ps[g, j][:], wq[j], P, 0, hq[g], 512)
+        def ls_pass(g, j):
+            ls_ps[g, j] = bank("A" + str(j), [P, GROUP])
+            mx_group(ls_ps[g, j][:], wls_q[j], P, 0, quantised[g])
 
-        def ex(g, j):
-            et_sb[g, j] = etp.tile([P, 512], F32, tag="et", name="et")
+        def exp_out(g, j):
+            exp_t[g, j] = exp_pool.tile([P, GROUP], F32, tag="exp_t", name="exp_t")
             nc.scalar.activation(
-                out=et_sb[g, j][:], in_=ls_ps[g, j][:], func=ACT.Exp, bias=half_bls[:, j : j + 1], scale=0.5
+                out=exp_t[g, j][:], in_=ls_ps[g, j][:], func=ACT.Exp, bias=half_bls[:, j : j + 1], scale=0.5
             )
 
-        def etr(g, j):
-            e_ps[g, j] = bank("A" + str(j), [P, T4, P])
-            for i in range(T4):
-                nc.tensor.transpose(e_ps[g, j][:, i, :], et_sb[g, j][:, i * P : (i + 1) * P], ident[:])
+        def exp_flip(g, j):
+            exp_ps[g, j] = bank("A" + str(j), [P, ROW_TILES, P])
+            for i in row_tiles:
+                nc.tensor.transpose(exp_ps[g, j][:, i, :], exp_t[g, j][:, i * P : (i + 1) * P], ident[:])
 
         def by_tile(t):
-            return t[:].rearrange("p (i n) -> p i n", i=T4)
+            return t[:].rearrange("p (i n) -> p i n", i=ROW_TILES)
 
-        def ph(g, j):
+        def times_eps(g, j):
             if g not in prod:
-                prod[g] = prodp.tile([P, T4 * XO], F32, tag="prod", name="prod")
+                prod[g] = prod_pool.tile([P, ROW_TILES * XO], F32, tag="prod", name="prod")
             cols = slice(j * P, (j + 1) * P)
             nc.vector.tensor_tensor(
-                out=by_tile(prod[g])[:, :, cols], in0=e_ps[g, j][:], in1=by_tile(eps_sb[g])[:, :, cols], op=ALU.mult
+                out=by_tile(prod[g])[:, :, cols], in0=exp_ps[g, j][:], in1=by_tile(eps_sb[g])[:, :, cols], op=ALU.mult
             )
 
-        def pc(g, j):
+        def plus_bmu(g, j):
             cols = slice(j * P, (j + 1) * P)
             nc.gpsimd.tensor_tensor(
-                out=by_tile(prod[g])[:, :, cols], in0=by_tile(prod[g])[:, :, cols], in1=by_tile(c4)[:, :, cols], op=ALU.add
+                out=by_tile(prod[g])[:, :, cols],
+                in0=by_tile(prod[g])[:, :, cols],
+                in1=by_tile(bmu_rows)[:, :, cols],
+                op=ALU.add,
             )
 
-        def mu(g, i):
+        def mu_pass(g, i):
             mu_ps[g, i] = bank("B" + str(i), [P, XO])
-            mx(mu_ps[g, i][:], hq[g], 512, i * P, hq["wmu"], 512)
+            mx_group(mu_ps[g, i][:], quantised[g], GROUP, i * P, quantised["wmu"])
 
-        def rs(g, i):
+        def plus_mu(g, i):
             if g not in res:
-                res[g] = resp.tile([P, T4 * XO], F32, tag="res", name="res")
+                res[g] = res_pool.tile([P, ROW_TILES * XO], F32, tag="res", name="res")
             cols = slice(i * XO, (i + 1) * XO)
             nc.vector.tensor_tensor(out=res[g][:, cols], in0=mu_ps[g, i][:], in1=prod[g][:, cols], op=ALU.add)
 
-        def store(g, i0, i1):
-            cols = slice(i0 * XO, i1 * XO)
-            nc.sync.dma_start(out=out_v[g][:, cols], in_=res[g][:, cols])
+        def store(g, first, end):
+            cols = slice(first * XO, end * XO)
+            nc.sync.dma_start(out=out_groups[g][:, cols], in_=res[g][:, cols])
 
-        R4 = range(T4)
+        def ls_and_exp(g):
+            for j in out_tiles:
+                ls_pass(g, j)
+            for j in out_tiles:
+                exp_out(g, j)
+
+        def exp_times_eps(g):
+            for j in out_tiles:
+                exp_flip(g, j)
+            for j in out_tiles:
+                times_eps(g, j)
+                plus_bmu(g, j)
+
         load_hd(0, True)
         load_w("wls", W_ls_d)
         load_hd(1, True)
@@ -237,88 +249,61 @@ def tile_vae_pb_t_kernel(tc, hd, W_mu_d, b_mu_d, W_ls_d, b_ls_d, eps_x, out):
             load_eps(g - 1)
         load_eps(GROUPS - 1)
 
-        for i in R4:
-            trh(0, i, "B" + str(i))
-            cph("VS"[i % 2], 0, i)
-        qh(0)
-        for r in R4:
-            trw("wls", r, "A" + str(r))
-            cp_wls(r)
-        q_wls(0)
-        q_wls(1)
-        q_wls(2)
-        bias_t()
-        bias_half()
-        q_wls(3)
-        for j in R4:
-            ls(0, j)
-        for j in R4:
-            ex(0, j)
-        bias_c4()
-        hb = ("B2", "B3", "B0", "B1")
-        for i in R4:
-            trh(1, i, hb[i])
-            cph("VS"[i % 2], 1, i)
-        qh(1)
-        for j in R4:
-            etr(0, j)
-        for j in R4:
-            ph(0, j)
-            pc(0, j)
-        for i in R4:
-            trh(2, i, hb[i])
-        for i in R4:
-            cph("S", 2, i)
-        for j in R4:
-            ls(1, j)
-        qh(2)
-        for j in R4:
-            ex(1, j)
-        for r in R4:
-            pend["wmu", r] = transpose_tile(w_sb["wmu"], r, hb[r])
-            cp_wmu("VS"[r % 2], r)
-        for j in R4:
-            etr(1, j)
-        for j in R4:
-            ph(1, j)
-            pc(1, j)
-        qh("wmu")
-        for i in R4:
-            trh(3, i, hb[i])
-        def mu_group(g, fine):
-            for i in R4:
-                mu(g, i)
-            for i in R4:
-                rs(g, i)
-                if fine:
-                    store(g, i, i + 1)
-            if not fine:
-                store(g, 0, T4)
+        for i in row_tiles:
+            flip(0, i, "B" + str(i))
+            regroup("VS"[i % 2], 0, i)
+        quantise(0)
+        for r in out_tiles:
+            flip("wls", r, "A" + str(r))
+            regroup_wls(r)
+        spread_biases()
+        for r in out_tiles:
+            if r == OUT_TILES - 1:
+                keep_half_bls()
+            quantise_wls(r)
 
-        def exp_back(g):
-            for j in R4:
-                etr(g, j)
-            for j in R4:
-                ph(g, j)
-                pc(g, j)
+        b_banks = ("B2", "B3", "B0", "B1")
+        ls_and_exp(0)
+        keep_bmu()
+        for i in row_tiles:
+            flip(1, i, b_banks[i])
+            regroup("VS"[i % 2], 1, i)
+        quantise(1)
+        exp_times_eps(0)
+        for i in row_tiles:
+            flip(2, i, b_banks[i])
+
+        for i in row_tiles:
+            regroup("S", 2, i)
+        quantise(2)
+        ls_and_exp(1)
+        for r in out_tiles:
+            flip("wmu", r, b_banks[r])
+            regroup("VS"[r % 2], "wmu", r)
+        exp_times_eps(1)
+        quantise("wmu")
+        for i in row_tiles:
+            flip(3, i, b_banks[i])
 
         for g in range(LAG, GROUPS):
             if g + 1 < GROUPS:
-                for i in R4:
-                    cph("S", g + 1, i)
-            for j in R4:
-                ls(g, j)
-            if g + 1 < GROUPS:
-                qh(g + 1)
-            for j in R4:
-                ex(g, j)
+                for i in row_tiles:
+                    regroup("S", g + 1, i)
+                quantise(g + 1)
+            ls_and_exp(g)
+            for i in row_tiles:
+                mu_pass(g - LAG, i)
+            for i in row_tiles:
+                plus_mu(g - LAG, i)
+            store(g - LAG, 0, ROW_TILES)
+            exp_times_eps(g)
             if g + 2 < GROUPS:
-                mu_group(g - LAG, False)
-                exp_back(g)
-                for i in R4:
-                    trh(g + 2, i, "B" + str(i))
-            else:
-                exp_back(g)
-                mu_group(g - LAG, g == GROUPS - 1)
+                for i in row_tiles:
+                    flip(g + 2, i, "B" + str(i))
+
         for g in range(GROUPS - LAG, GROUPS):
-            mu_group(g, True)
+            for i in row_tiles:
+                mu_pass(g, i)
+            for i in row_tiles:
+                plus_mu(g, i)
+                store(g, i, i + 1)

from contextlib import ExitStack

import concourse.mybir as mybir
from concourse.masks import make_identity

F32 = mybir.dt.float32
BF16 = mybir.dt.bfloat16
U32 = mybir.dt.uint32
U8 = mybir.dt.uint8
FP8X4 = mybir.dt.float8_e4m3fn_x4
ACT = mybir.ActivationFunctionType
ALU = mybir.AluOpType

P = 128
B, K, XO = 4096, 1024, 512
MOVING = 512
GROUP = MOVING
GROUPS = B // GROUP
ROW_TILES = GROUP // P
OUT_TILES = XO // P
PACK = 4
K_PASS = 512
PASSES = K // K_PASS
WORDS = K // 2
PLANES = WORDS // P
LAG = 2
FLOPS = 2 * B * K * 2 * XO

assert XO == MOVING
assert OUT_TILES == ROW_TILES


def tile_vae_pb_t_kernel(tc, hd, W_mu_d, b_mu_d, W_ls_d, b_ls_d, eps_x, out):
    nc = tc.nc
    hd_groups = hd.rearrange("(g p i) k -> g p (i k)", p=P, i=ROW_TILES)
    hd_tiles = hd.rearrange("(g p i) k -> g i p k", p=P, i=ROW_TILES)
    eps_groups = eps_x.rearrange("(g p i) n -> g p (i n)", p=P, i=ROW_TILES)
    out_groups = out.rearrange("(g p i) n -> g p (i n)", p=P, i=ROW_TILES)
    row_tiles = range(ROW_TILES)
    out_tiles = range(OUT_TILES)

    with ExitStack() as ctx:
        const = ctx.enter_context(tc.tile_pool(name="const", bufs=1))
        raw = ctx.enter_context(tc.tile_pool(name="raw", bufs=4))
        eps_pool = ctx.enter_context(tc.tile_pool(name="eps", bufs=GROUPS))
        qin_pool = ctx.enter_context(tc.tile_pool(name="quant_in", bufs=2))
        wls_pool = ctx.enter_context(tc.tile_pool(name="wls_in", bufs=OUT_TILES))
        code_pool = ctx.enter_context(tc.tile_pool(name="hd_codes", bufs=5))
        exp_pool = ctx.enter_context(tc.tile_pool(name="exp_t", bufs=OUT_TILES))
        prod_pool = ctx.enter_context(tc.tile_pool(name="prod", bufs=4))
        res_pool = ctx.enter_context(tc.tile_pool(name="res", bufs=3))
        psum = ctx.enter_context(tc.psum_pool(name="psum", bufs=1))
        ctx.enter_context(tc.manual_schedule())

        def bank(tag, shape, dtype=F32):
            return psum.tile(shape, dtype, tag=tag, name="ps" + tag)

        ident = const.tile([P, P], F32, name="ident")
        make_identity(nc, ident[:])
        ident_bf = const.tile([P, P], BF16, name="ident_bf")
        make_identity(nc, ident_bf[:])
        brow_mu = const.tile([P, XO], BF16, name="brow_mu")
        nc.vector.memset(brow_mu[:], 0.0)
        bcol = const.tile([P, P], BF16, name="bcol")
        nc.vector.memset(bcol[:], 0.0)
        ones = const.tile([P, P], BF16, name="ones")
        nc.vector.memset(ones[:], 1.0)
        warm = const.tile([P, 1], F32, name="warm")
        nc.vector.memset(warm[:], 0.0)
        nc.scalar.dma_start(out=bcol[0:OUT_TILES, :], in_=b_ls_d.rearrange("(j q) -> j q", q=P))
        nc.scalar.dma_start(out=brow_mu[0:1, :], in_=b_mu_d.rearrange("(o n) -> o n", o=1))
        warm2 = const.tile([P, 1], F32, name="warm2")
        nc.scalar.activation(out=warm2[:], in_=warm[:], func=ACT.Exp)

        loaded, eps_sb = {}, {}
        flipped = {}
        quant_in, quantised = {}, {}
        wls_in, wls_q = {}, {}
        ls_ps, exp_t, exp_ps, mu_ps, prod, res = {}, {}, {}, {}, {}, {}
        bias_ps = {}

        def load_hd(g, in_tiles):
            t = raw.tile([P, ROW_TILES * K], BF16, tag="raw", name="hd_sb")
            if in_tiles:
                for i in row_tiles:
                    nc.sync.dma_start(out=t[:, i * K : (i + 1) * K], in_=hd_tiles[g, i])
            else:
                nc.sync.dma_start(out=t[:], in_=hd_groups[g])
            loaded[g] = t

        def load_w(name, w):
            t = const.tile([P, OUT_TILES * K], BF16, name=name)
            for r in out_tiles:
                nc.sync.dma_start(out=t[:, r * K : (r + 1) * K], in_=w[r * P : (r + 1) * P, :])
            loaded[name] = t

        def load_eps(g):
            t = eps_pool.tile([P, ROW_TILES * XO], BF16, tag="eps", name="eps_sb")
            nc.sync.dma_start(out=t[:], in_=eps_groups[g])
            eps_sb[g] = t

        def flip(g, i, tag):
            words = loaded[g][:].bitcast(F32)
            bk = bank(tag, [P, PLANES, P])
            for s in range(PLANES):
                c0 = i * WORDS + s * P
                nc.tensor.transpose(bk[:, s, :], words[:, c0 : c0 + P], ident[:])
            flipped[g, i] = bk

        def copy_out(engine, dst, bk):
            src = bk[:].rearrange("p (c u) n -> p c n u", u=2)
            if engine == "V":
                nc.vector.tensor_copy(out=dst, in_=src)
            else:
                nc.scalar.copy(out=dst, in_=src)

        def as_words(t):
            return t[:].bitcast(F32).rearrange("p (c n u) -> p c n u", c=PASSES, u=2)

        def regroup(engine, g, i):
            if g not in quant_in:
                quant_in[g] = qin_pool.tile([P, ROW_TILES * K], BF16, tag="quant_in", name="quant_in", align_bytes=64)
            copy_out(engine, as_words(quant_in[g])[:, :, i * P : (i + 1) * P, :], flipped[g, i])

        def quantise(g):
            pool, tag = (const, "wmu") if g == "wmu" else (code_pool, "hd")
            codes = pool.tile([P, PASSES * MOVING], U32, tag=tag + "c", name=tag + "c", align_bytes=64)
            scales = pool.tile([P, PASSES * MOVING], U8, tag=tag + "s", name=tag + "s", align_bytes=64)
            for c in range(PASSES):
                nc.vector.quantize_mx(
                    out=codes[:, c * MOVING : (c + 1) * MOVING].bitcast(FP8X4),
                    scales=scales[:, c * MOVING : (c + 1) * MOVING],
                    in_=quant_in[g][:, c * PACK * MOVING : (c + 1) * PACK * MOVING],
                )
            quantised[g] = (codes, scales)

        def regroup_wls(r):
            t = wls_pool.tile([P, K], BF16, tag="wls_in", name="wls_in", align_bytes=64)
            copy_out("S", as_words(t), flipped["wls", r])
            wls_in[r] = t

        def quantise_wls(r):
            codes = const.tile([P, PASSES * P], U32, name="wlsc" + str(r), align_bytes=64)
            scales = const.tile([P, PASSES * P], U8, name="wlss" + str(r), align_bytes=64)
            nc.vector.quantize_mx(out=codes[:].bitcast(FP8X4), scales=scales[:], in_=wls_in[r][:])
            wls_q[r] = (codes, scales)

        def mx_group(acc, stationary, pitch, first, moving):
            for c in range(PASSES):
                a = c * pitch + first
                b = c * MOVING
                nc.tensor.matmul_mx(
                    out=acc,
                    lhsT=stationary[0][:, a : a + P].bitcast(FP8X4),
                    lhsT_scale=stationary[1][:, a : a + P],
                    rhs=moving[0][:, b : b + MOVING].bitcast(FP8X4),
                    rhs_scale=moving[1][:, b : b + MOVING],
                    start=(c == 0),
                    stop=(c == PASSES - 1),
                )

        def spread_biases():
            bias_ps["ls"] = bank("B0", [P, P], BF16)
            nc.tensor.transpose(bias_ps["ls"][:], bcol[:], ident_bf[:])
            bias_ps["mu"] = bank("B1", [P, XO])
            nc.tensor.matmul(out=bias_ps["mu"][:], lhsT=ones[:], rhs=brow_mu[:], start=True, stop=True)

        half_bls = const.tile([P, OUT_TILES], F32, name="half_bls")
        bmu_rows = const.tile([P, ROW_TILES * XO], F32, name="bmu_rows")

        def keep_half_bls():
            nc.vector.tensor_scalar_mul(out=half_bls[:], in0=bias_ps["ls"][:, 0:OUT_TILES], scalar1=0.5)

        def keep_bmu():
            for i in row_tiles:
                nc.vector.tensor_copy(out=bmu_rows[:, i * XO : (i + 1) * XO], in_=bias_ps["mu"][:])

        def ls_pass(g, j):
            ls_ps[g, j] = bank("A" + str(j), [P, GROUP])
            mx_group(ls_ps[g, j][:], wls_q[j], P, 0, quantised[g])

        def exp_out(g, j):
            exp_t[g, j] = exp_pool.tile([P, GROUP], F32, tag="exp_t", name="exp_t")
            nc.scalar.activation(
                out=exp_t[g, j][:], in_=ls_ps[g, j][:], func=ACT.Exp, bias=half_bls[:, j : j + 1], scale=0.5
            )

        def exp_flip(g, j):
            exp_ps[g, j] = bank("A" + str(j), [P, ROW_TILES, P])
            for i in row_tiles:
                nc.tensor.transpose(exp_ps[g, j][:, i, :], exp_t[g, j][:, i * P : (i + 1) * P], ident[:])

        def by_tile(t):
            return t[:].rearrange("p (i n) -> p i n", i=ROW_TILES)

        def times_eps(g, j):
            if g not in prod:
                prod[g] = prod_pool.tile([P, ROW_TILES * XO], F32, tag="prod", name="prod")
            cols = slice(j * P, (j + 1) * P)
            nc.vector.tensor_tensor(
                out=by_tile(prod[g])[:, :, cols], in0=exp_ps[g, j][:], in1=by_tile(eps_sb[g])[:, :, cols], op=ALU.mult
            )

        def plus_bmu(g, j):
            cols = slice(j * P, (j + 1) * P)
            nc.gpsimd.tensor_tensor(
                out=by_tile(prod[g])[:, :, cols],
                in0=by_tile(prod[g])[:, :, cols],
                in1=by_tile(bmu_rows)[:, :, cols],
                op=ALU.add,
            )

        def mu_pass(g, i):
            mu_ps[g, i] = bank("B" + str(i), [P, XO])
            mx_group(mu_ps[g, i][:], quantised[g], GROUP, i * P, quantised["wmu"])

        def plus_mu(g, i):
            if g not in res:
                res[g] = res_pool.tile([P, ROW_TILES * XO], F32, tag="res", name="res")
            cols = slice(i * XO, (i + 1) * XO)
            nc.vector.tensor_tensor(out=res[g][:, cols], in0=mu_ps[g, i][:], in1=prod[g][:, cols], op=ALU.add)

        def store(g, first, end):
            cols = slice(first * XO, end * XO)
            nc.sync.dma_start(out=out_groups[g][:, cols], in_=res[g][:, cols])

        def ls_and_exp(g):
            for j in out_tiles:
                ls_pass(g, j)
            for j in out_tiles:
                exp_out(g, j)

        def exp_times_eps(g):
            for j in out_tiles:
                exp_flip(g, j)
            for j in out_tiles:
                times_eps(g, j)
                plus_bmu(g, j)

        load_hd(0, True)
        load_w("wls", W_ls_d)
        load_hd(1, True)
        load_eps(0)
        load_hd(2, False)
        load_w("wmu", W_mu_d)
        load_eps(1)
        for g in range(3, GROUPS):
            load_hd(g, False)
            load_eps(g - 1)
        load_eps(GROUPS - 1)

        for i in row_tiles:
            flip(0, i, "B" + str(i))
            regroup("VS"[i % 2], 0, i)
        quantise(0)
        for r in out_tiles:
            flip("wls", r, "A" + str(r))
            regroup_wls(r)
        spread_biases()
        for r in out_tiles:
            if r == OUT_TILES - 1:
                keep_half_bls()
            quantise_wls(r)

        b_banks = ("B2", "B3", "B0", "B1")
        ls_and_exp(0)
        keep_bmu()
        for i in row_tiles:
            flip(1, i, b_banks[i])
            regroup("VS"[i % 2], 1, i)
        quantise(1)
        exp_times_eps(0)
        for i in row_tiles:
            flip(2, i, b_banks[i])

        for i in row_tiles:
            regroup("S", 2, i)
        quantise(2)
        ls_and_exp(1)
        for r in out_tiles:
            flip("wmu", r, b_banks[r])
            regroup("VS"[r % 2], "wmu", r)
        exp_times_eps(1)
        quantise("wmu")
        for i in row_tiles:
            flip(3, i, b_banks[i])

        for g in range(LAG, GROUPS):
            if g + 1 < GROUPS:
                for i in row_tiles:
                    regroup("S", g + 1, i)
                quantise(g + 1)
            ls_and_exp(g)
            for i in row_tiles:
                mu_pass(g - LAG, i)
            for i in row_tiles:
                plus_mu(g - LAG, i)
            store(g - LAG, 0, ROW_TILES)
            exp_times_eps(g)
            if g + 2 < GROUPS:
                for i in row_tiles:
                    flip(g + 2, i, "B" + str(i))

        for g in range(GROUPS - LAG, GROUPS):
            for i in row_tiles:
                mu_pass(g, i)
            for i in row_tiles:
                plus_mu(g, i)
                store(g, i, i + 1)
